import numpy as np
import ml_dtypes


def mxq(x, axis, fmt="e4m3"):
    dtype, down = {"e4m3": (ml_dtypes.float8_e4m3fn, 7), "e5m2": (ml_dtypes.float8_e5m2, 14)}[fmt]
    v = np.moveaxis(np.asarray(x, np.float32).astype(ml_dtypes.bfloat16).astype(np.float64), axis, -1)
    blocks = v.reshape(v.shape[:-1] + (-1, 32))
    amax = np.abs(blocks).max(-1, keepdims=True)
    byte = np.maximum(np.where(amax > 0, np.frexp(amax)[1] - 1 + 127, 0) - down, 1)
    scale = np.exp2(byte - 127.0)
    codes = (blocks / scale).astype(np.float32).astype(dtype).astype(np.float64)
    return np.moveaxis((codes * scale).reshape(v.shape), -1, axis)


WIDE = False


def mx_kscale(k):
    if not WIDE:
        return np.ones(k)
    levels = np.array([10, -10, 5, -5, 0])
    if k % 512:
        return np.exp2(np.random.permutation(np.resize(levels, k // 32))).repeat(32)
    a = np.empty((k // 512, 16))
    for p in range(k // 512):
        a[p, :8] = np.random.permutation(np.resize(levels, 8))
        for g in range(8):
            far = levels[np.abs(levels - a[p, g]) >= 10]
            a[p, g + 8] = far[np.random.randint(len(far))]
    return np.exp2(a.ravel()).repeat(32)


BF16 = ml_dtypes.bfloat16


def bf(x):
    return np.asarray(x, np.float32).astype(BF16)


def f64(x):
    return np.asarray(x).astype(np.float64)


B, N, I, O = 2, 512, 256, 128


def setup_inputs():
    s = mx_kscale(N)
    limit = np.sqrt(6.0 / (I + O))
    return {"seq": bf(np.random.standard_normal((B, N, I)) / s[None, :, None]),
            "adj": bf(np.random.uniform(0.0, 1.0, (B, N, N)) / np.sqrt(N) * s[None, None, :]),
            "W": bf(np.random.uniform(-limit, limit, (O, I))),
            "b": bf(np.random.standard_normal(O) * 0.1 / s.max()),
            "alpha": bf(0.25 + 0.05 * np.random.standard_normal(1))}


def reference(seq, adj, W, b, alpha):
    h = f64(seq) @ f64(W).T + f64(b)
    h = mxq(f64(adj), 2, "e4m3") @ mxq(h, 1, "e4m3")
    return np.where(h > 0, h, f64(alpha) * h)

@@ -1,0 +1,220 @@
+from contextlib import ExitStack
+
+import concourse.mybir as mybir
+from concourse.masks import make_identity
+
+F32 = mybir.dt.float32
+BF16 = mybir.dt.bfloat16
+U32 = mybir.dt.uint32
+U8 = mybir.dt.uint8
+FP8X4 = mybir.dt.float8_e4m3fn_x4
+ALU = mybir.AluOpType
+ACT = mybir.ActivationFunctionType
+
+P = 128
+PACK = 4
+GRAPHS, NODES, F_IN, F_OUT = 2, 512, 256, 128
+ROW_TILES = NODES // P
+HALVES = 2 * GRAPHS
+TILES_PER_HALF = ROW_TILES // 2
+BANK = 512
+WARM_PASSES = 12
+
+FLOPS = 2 * GRAPHS * NODES * F_IN * F_OUT + 2 * GRAPHS * NODES * NODES * F_OUT
+
+
+def tile_gcn_s_kernel(tc, seq, adj, W, b, alpha, out):
+    nc = tc.nc
+    with ExitStack() as ctx:
+        ctx.enter_context(tc.manual_schedule())
+        const = ctx.enter_context(tc.tile_pool(name="const", bufs=1))
+        per_graph = ctx.enter_context(tc.tile_pool(name="per_graph", bufs=GRAPHS))
+        per_half = ctx.enter_context(tc.tile_pool(name="per_half", bufs=HALVES))
+        psum_t = ctx.enter_context(tc.psum_pool(name="psum_t", bufs=3))
+        psum_acc = ctx.enter_context(tc.psum_pool(name="psum_acc", bufs=4))
+        psum_small = ctx.enter_context(tc.psum_pool(name="psum_small", bufs=1))
+
+        small_row = const.tile([P, 2 * F_OUT], BF16)
+        nc.gpsimd.memset(small_row[:], 0.0)
+        zero_col = const.tile([P, 1], F32)
+        nc.gpsimd.memset(zero_col[:], 0.0)
+        ident = const.tile([P, P], F32)
+        make_identity(nc, ident[:])
+
+        warm_zeros = const.tile([P, P * PACK], BF16, align_bytes=64)
+        nc.vector.memset(warm_zeros[:], 0.0)
+        warm_codes = const.tile([P, P], U32, align_bytes=64)
+        warm_scales = const.tile([P, P], U8, align_bytes=64)
+        nc.vector.quantize_mx(out=warm_codes[:].bitcast(FP8X4), scales=warm_scales[:], in_=warm_zeros[:])
+        warm_ps = psum_t.tile([P, BANK], F32, tag="transposed")
+        for i in range(WARM_PASSES):
+            nc.tensor.matmul_mx(
+                out=warm_ps[:, 0:P],
+                lhsT=warm_codes[:].bitcast(FP8X4),
+                lhsT_scale=warm_scales[:],
+                rhs=warm_codes[:].bitcast(FP8X4),
+                rhs_scale=warm_scales[:],
+                start=True,
+                stop=True,
+            )
+
+        w_rows = const.tile([P, F_IN], BF16)
+        nc.sync.dma_start(out=w_rows[:], in_=W[:, :])
+        nc.scalar.dma_start(out=small_row[0:1, 0:F_OUT], in_=b.unsqueeze(0))
+        nc.scalar.dma_start(out=small_row[0:1, F_OUT : F_OUT + 1], in_=alpha.unsqueeze(0))
+
+        seq_rows_of = []
+        for k in range(HALVES):
+            seq_rows = per_half.tile([P, 2 * F_IN], BF16)
+            seq_view = seq[k // 2].rearrange("(p t) i -> p (t i)", t=PACK)
+            first = (k % 2) * 2 * F_IN
+            nc.sync.dma_start(out=seq_rows[:], in_=seq_view[:, first : first + 2 * F_IN])
+            seq_rows_of.append(seq_rows)
+
+        adj_rows_of = []
+        for k in range(HALVES):
+            adj_rows = per_half.tile([P, TILES_PER_HALF * NODES], BF16)
+            adj_view = adj[k // 2].rearrange("(p j) m -> p (j m)", j=ROW_TILES)
+            first = (k % 2) * TILES_PER_HALF * NODES
+            nc.sync.dma_start(out=adj_rows[:], in_=adj_view[:, first : first + TILES_PER_HALF * NODES])
+            adj_rows_of.append(adj_rows)
+
+        ones = const.tile([P, P], BF16)
+        nc.scalar.activation(
+            out=ones[:], in_=zero_col[:, 0:1].to_broadcast([P, P]), func=ACT.Relu, scale=0.0, bias=1.0
+        )
+
+        w_t_ps = psum_t.tile([P, BANK], F32, tag="transposed")
+        nc.tensor.transpose(w_t_ps[:, 0:P], w_rows[:].bitcast(F32), ident[:])
+        w_t = const.tile([P, F_OUT], F32)
+        nc.scalar.copy(out=w_t[:], in_=w_t_ps[:, 0:P])
+        w_pairs = w_t[:].bitcast(BF16).rearrange("p (o r) -> p o r", r=2)
+
+        seq_t_of = []
+        for k in range(HALVES):
+            seq_words = seq_rows_of[k][:].bitcast(F32)
+            seq_t_ps = psum_t.tile([P, BANK], F32, tag="transposed")
+            for e in range(2):
+                cols = slice(e * P, (e + 1) * P)
+                nc.tensor.transpose(seq_t_ps[:, cols], seq_words[:, cols], ident[:])
+            seq_t = per_half.tile([P, 2 * P], F32)
+            if k % 2 == 0:
+                nc.vector.tensor_copy(out=seq_t[:], in_=seq_t_ps[:, 0 : 2 * P])
+            else:
+                nc.scalar.copy(out=seq_t[:], in_=seq_t_ps[:, 0 : 2 * P])
+            seq_t_of.append(seq_t)
+
+        small_ps = psum_small.tile([P, 2 * F_OUT], F32)
+        nc.tensor.matmul(small_ps[:], lhsT=ones[:], rhs=small_row[:], start=True, stop=True)
+        bias_all = const.tile([P, F_OUT], F32)
+        nc.vector.tensor_copy(out=bias_all[:], in_=small_ps[:, 0:F_OUT])
+        one_minus_alpha = const.tile([P, 1], F32)
+        nc.vector.tensor_scalar(
+            out=one_minus_alpha[:],
+            in0=small_ps[:, F_OUT : F_OUT + 1],
+            scalar1=-1.0,
+            scalar2=1.0,
+            op0=ALU.mult,
+            op1=ALU.add,
+        )
+
+        h_grouped_of = []
+        h_codes_of = []
+        h_scales_of = []
+        adj_grouped_of = []
+        adj_codes_of = []
+        adj_scales_of = []
+
+        def project(g):
+            h_ps = psum_acc.tile([P, PACK * F_OUT], F32, tag="acc")
+            for t in range(PACK):
+                seq_pairs = seq_t_of[2 * g + t // 2][:].bitcast(BF16).rearrange(
+                    "p (e c r) -> p e c r", e=2, r=2
+                )
+                for r in range(2):
+                    nc.tensor.matmul(
+                        h_ps[:, t * F_OUT : (t + 1) * F_OUT],
+                        lhsT=seq_pairs[:, t % 2, :, r],
+                        rhs=w_pairs[:, :, r],
+                        start=(r == 0),
+                        stop=(r == 1),
+                    )
+            h_grouped = per_graph.tile([P, F_OUT * PACK], BF16, align_bytes=64)
+            nc.vector.tensor_tensor(
+                out=h_grouped[:].rearrange("p (o t) -> p o t", t=PACK),
+                in0=h_ps[:].rearrange("p (t o) -> p o t", t=PACK),
+                in1=bias_all[:].unsqueeze(2).to_broadcast([P, F_OUT, PACK]),
+                op=ALU.add,
+            )
+            h_grouped_of.append(h_grouped)
+
+        def transpose_adj(k):
+            adj_words = adj_rows_of[k][:].bitcast(F32)
+            adj_t_ps = psum_t.tile([P, BANK], F32, tag="transposed")
+            for j in range(TILES_PER_HALF):
+                for u in range(2):
+                    block = 2 * j + u
+                    nc.tensor.transpose(
+                        adj_t_ps[:, block * P : (block + 1) * P],
+                        adj_words[:, j * 2 * P + u : (j + 1) * 2 * P : 2],
+                        ident[:],
+                    )
+            adj_grouped = per_half.tile([P, TILES_PER_HALF * P * PACK], BF16, align_bytes=64)
+            nc.scalar.copy(
+                out=adj_grouped[:].bitcast(F32).rearrange("p (j c u) -> p j c u", j=TILES_PER_HALF, u=2),
+                in_=adj_t_ps[:].rearrange("p (j u c) -> p j c u", j=TILES_PER_HALF, u=2),
+            )
+            adj_grouped_of.append(adj_grouped)
+
+        def quantise(k):
+            adj_codes = per_half.tile([P, TILES_PER_HALF * P], U32, align_bytes=64)
+            adj_scales = per_half.tile([P, TILES_PER_HALF * P], U8, align_bytes=64)
+            nc.vector.quantize_mx(
+                out=adj_codes[:].bitcast(FP8X4), scales=adj_scales[:], in_=adj_grouped_of[k][:]
+            )
+            adj_codes_of.append(adj_codes)
+            adj_scales_of.append(adj_scales)
+            if k % 2 == 0:
+                h_codes = per_graph.tile([P, F_OUT], U32, align_bytes=64)
+                h_scales = per_graph.tile([P, F_OUT], U8, align_bytes=64)
+                nc.vector.quantize_mx(
+                    out=h_codes[:].bitcast(FP8X4), scales=h_scales[:], in_=h_grouped_of[k // 2][:]
+                )
+                h_codes_of.append(h_codes)
+                h_scales_of.append(h_scales)
+
+        for k in range(HALVES):
+            if k % 2 == 0:
+                project(k // 2)
+            transpose_adj(k)
+            if k >= 1:
+                quantise(k - 1)
+        quantise(HALVES - 1)
+
+        for k in range(HALVES):
+            g = k // 2
+            a_ps = psum_acc.tile([P, TILES_PER_HALF * F_OUT], F32, tag="acc")
+            for j in range(TILES_PER_HALF):
+                nc.tensor.matmul_mx(
+                    out=a_ps[:, j * F_OUT : (j + 1) * F_OUT],
+                    lhsT=adj_codes_of[k][:, j * P : (j + 1) * P].bitcast(FP8X4),
+                    lhsT_scale=adj_scales_of[k][:, j * P : (j + 1) * P],
+                    rhs=h_codes_of[g][:].bitcast(FP8X4),
+                    rhs_scale=h_scales_of[g][:],
+                    start=True,
+                    stop=True,
+                )
+            neg_part = per_half.tile([P, TILES_PER_HALF * F_OUT], F32)
+            nc.scalar.activation(out=neg_part[:], in_=a_ps[:], func=ACT.Relu, scale=-1.0)
+            result = per_half.tile([P, TILES_PER_HALF * F_OUT], F32)
+            nc.vector.scalar_tensor_tensor(
+                out=result[:],
+                in0=neg_part[:],
+                scalar=one_minus_alpha[:, 0:1],
+                in1=a_ps[:],
+                op0=ALU.mult,
+                op1=ALU.add,
+            )
+            out_view = out[g].rearrange("(p j) o -> p (j o)", j=ROW_TILES)
+            first = (k % 2) * TILES_PER_HALF * F_OUT
+            nc.sync.dma_start(out=out_view[:, first : first + TILES_PER_HALF * F_OUT], in_=result[:])

@@ -18,7 +18,8 @@ ROW_TILES = NODES // P
 HALVES = 2 * GRAPHS
 TILES_PER_HALF = ROW_TILES // 2
 BANK = 512
-WARM_PASSES = 12
+WARM_HEAD = 7
+WARM_GAP = 3
 
 FLOPS = 2 * GRAPHS * NODES * F_IN * F_OUT + 2 * GRAPHS * NODES * NODES * F_OUT
 
@@ -30,9 +31,33 @@ def tile_gcn_s_kernel(tc, seq, adj, W, b, alpha, out):
         const = ctx.enter_context(tc.tile_pool(name="const", bufs=1))
         per_graph = ctx.enter_context(tc.tile_pool(name="per_graph", bufs=GRAPHS))
         per_half = ctx.enter_context(tc.tile_pool(name="per_half", bufs=HALVES))
-        psum_t = ctx.enter_context(tc.psum_pool(name="psum_t", bufs=3))
+        psum_t = ctx.enter_context(tc.psum_pool(name="psum_t", bufs=4))
         psum_acc = ctx.enter_context(tc.psum_pool(name="psum_acc", bufs=4))
-        psum_small = ctx.enter_context(tc.psum_pool(name="psum_small", bufs=1))
+
+        b_alpha = const.tile([1, F_OUT + 1], BF16)
+        nc.scalar.dma_start(out=b_alpha[:, 0:F_OUT], in_=b.unsqueeze(0))
+        nc.scalar.dma_start(out=b_alpha[:, F_OUT : F_OUT + 1], in_=alpha.unsqueeze(0))
+        w_rows = const.tile([P, F_IN], BF16)
+        nc.sync.dma_start(out=w_rows[:], in_=W[:, :])
+        seq_rows_of = []
+        adj_rows_of = []
+        for g in range(GRAPHS):
+            seq_rows = per_graph.tile([P, PACK * F_IN], BF16)
+            nc.sync.dma_start(out=seq_rows[:], in_=seq[g].rearrange("(p t) i -> p (t i)", t=PACK))
+            seq_rows_of.append(seq_rows)
+        for g in range(GRAPHS):
+            adj_view = adj[g].rearrange("(p j) m -> p (j m)", j=ROW_TILES)
+            for half in range(2):
+                adj_rows = per_half.tile([P, TILES_PER_HALF * NODES], BF16)
+                first = half * TILES_PER_HALF * NODES
+                nc.sync.dma_start(out=adj_rows[:], in_=adj_view[:, first : first + TILES_PER_HALF * NODES])
+                adj_rows_of.append(adj_rows)
+
+        warm_zeros = const.tile([P, P * PACK], BF16, align_bytes=64)
+        nc.vector.memset(warm_zeros[:].bitcast(F32), 0.0)
+        warm_codes = const.tile([P, P], U32, align_bytes=64)
+        warm_scales = const.tile([P, P], U8, align_bytes=64)
+        nc.vector.quantize_mx(out=warm_codes[:].bitcast(FP8X4), scales=warm_scales[:], in_=warm_zeros[:])
 
         small_row = const.tile([P, 2 * F_OUT], BF16)
         nc.gpsimd.memset(small_row[:], 0.0)
@@ -40,90 +65,44 @@ def tile_gcn_s_kernel(tc, seq, adj, W, b, alpha, out):
         nc.gpsimd.memset(zero_col[:], 0.0)
         ident = const.tile([P, P], F32)
         make_identity(nc, ident[:])
-
-        warm_zeros = const.tile([P, P * PACK], BF16, align_bytes=64)
-        nc.vector.memset(warm_zeros[:], 0.0)
-        warm_codes = const.tile([P, P], U32, align_bytes=64)
-        warm_scales = const.tile([P, P], U8, align_bytes=64)
-        nc.vector.quantize_mx(out=warm_codes[:].bitcast(FP8X4), scales=warm_scales[:], in_=warm_zeros[:])
-        warm_ps = psum_t.tile([P, BANK], F32, tag="transposed")
-        for i in range(WARM_PASSES):
-            nc.tensor.matmul_mx(
-                out=warm_ps[:, 0:P],
-                lhsT=warm_codes[:].bitcast(FP8X4),
-                lhsT_scale=warm_scales[:],
-                rhs=warm_codes[:].bitcast(FP8X4),
-                rhs_scale=warm_scales[:],
-                start=True,
-                stop=True,
-            )
-
-        w_rows = const.tile([P, F_IN], BF16)
-        nc.sync.dma_start(out=w_rows[:], in_=W[:, :])
-        nc.scalar.dma_start(out=small_row[0:1, 0:F_OUT], in_=b.unsqueeze(0))
-        nc.scalar.dma_start(out=small_row[0:1, F_OUT : F_OUT + 1], in_=alpha.unsqueeze(0))
-
-        seq_rows_of = []
-        for k in range(HALVES):
-            seq_rows = per_half.tile([P, 2 * F_IN], BF16)
-            seq_view = seq[k // 2].rearrange("(p t) i -> p (t i)", t=PACK)
-            first = (k % 2) * 2 * F_IN
-            nc.sync.dma_start(out=seq_rows[:], in_=seq_view[:, first : first + 2 * F_IN])
-            seq_rows_of.append(seq_rows)
-
-        adj_rows_of = []
-        for k in range(HALVES):
-            adj_rows = per_half.tile([P, TILES_PER_HALF * NODES], BF16)
-            adj_view = adj[k // 2].rearrange("(p j) m -> p (j m)", j=ROW_TILES)
-            first = (k % 2) * TILES_PER_HALF * NODES
-            nc.sync.dma_start(out=adj_rows[:], in_=adj_view[:, first : first + TILES_PER_HALF * NODES])
-            adj_rows_of.append(adj_rows)
-
         ones = const.tile([P, P], BF16)
         nc.scalar.activation(
             out=ones[:], in_=zero_col[:, 0:1].to_broadcast([P, P]), func=ACT.Relu, scale=0.0, bias=1.0
         )
 
-        w_t_ps = psum_t.tile([P, BANK], F32, tag="transposed")
-        nc.tensor.transpose(w_t_ps[:, 0:P], w_rows[:].bitcast(F32), ident[:])
-        w_t = const.tile([P, F_OUT], F32)
-        nc.scalar.copy(out=w_t[:], in_=w_t_ps[:, 0:P])
-        w_pairs = w_t[:].bitcast(BF16).rearrange("p (o r) -> p o r", r=2)
+        warm_ps = psum_acc.tile([P, BANK], F32, tag="acc")
+
+        def warm(passes):
+            for i in range(passes):
+                nc.tensor.matmul_mx(
+                    out=warm_ps[:, 0:P],
+                    lhsT=warm_codes[:].bitcast(FP8X4),
+                    lhsT_scale=warm_scales[:],
+                    rhs=warm_codes[:].bitcast(FP8X4),
+                    rhs_scale=warm_scales[:],
+                    start=True,
+                    stop=True,
+                )
 
         seq_t_of = []
-        for k in range(HALVES):
-            seq_words = seq_rows_of[k][:].bitcast(F32)
-            seq_t_ps = psum_t.tile([P, BANK], F32, tag="transposed")
-            for e in range(2):
-                cols = slice(e * P, (e + 1) * P)
-                nc.tensor.transpose(seq_t_ps[:, cols], seq_words[:, cols], ident[:])
-            seq_t = per_half.tile([P, 2 * P], F32)
-            if k % 2 == 0:
-                nc.vector.tensor_copy(out=seq_t[:], in_=seq_t_ps[:, 0 : 2 * P])
-            else:
-                nc.scalar.copy(out=seq_t[:], in_=seq_t_ps[:, 0 : 2 * P])
-            seq_t_of.append(seq_t)
-
-        small_ps = psum_small.tile([P, 2 * F_OUT], F32)
-        nc.tensor.matmul(small_ps[:], lhsT=ones[:], rhs=small_row[:], start=True, stop=True)
-        bias_all = const.tile([P, F_OUT], F32)
-        nc.vector.tensor_copy(out=bias_all[:], in_=small_ps[:, 0:F_OUT])
-        one_minus_alpha = const.tile([P, 1], F32)
-        nc.vector.tensor_scalar(
-            out=one_minus_alpha[:],
-            in0=small_ps[:, F_OUT : F_OUT + 1],
-            scalar1=-1.0,
-            scalar2=1.0,
-            op0=ALU.mult,
-            op1=ALU.add,
-        )
-
         h_grouped_of = []
         h_codes_of = []
         h_scales_of = []
-        adj_grouped_of = []
-        adj_codes_of = []
-        adj_scales_of = []
+        adj_codes_of = {}
+        adj_scales_of = {}
+
+        def transpose_seq(g, copies):
+            seq_words = seq_rows_of[g][:].bitcast(F32)
+            for u in range(2):
+                seq_t_ps = psum_t.tile([P, BANK], F32, tag="transposed")
+                for e in range(2):
+                    t = 2 * u + e
+                    nc.tensor.transpose(
+                        seq_t_ps[:, e * P : (e + 1) * P], seq_words[:, t * P : (t + 1) * P], ident[:]
+                    )
+                seq_t = per_half.tile([P, 2 * P], F32)
+                copies[u](out=seq_t[:], in_=seq_t_ps[:, 0 : 2 * P])
+                seq_t_of.append(seq_t)
 
         def project(g):
             h_ps = psum_acc.tile([P, PACK * F_OUT], F32, tag="acc")
@@ -139,6 +118,9 @@ def tile_gcn_s_kernel(tc, seq, adj, W, b, alpha, out):
                         start=(r == 0),
                         stop=(r == 1),
                     )
+            return h_ps
+
+        def add_bias(h_ps):
             h_grouped = per_graph.tile([P, F_OUT * PACK], BF16, align_bytes=64)
             nc.vector.tensor_tensor(
                 out=h_grouped[:].rearrange("p (o t) -> p o t", t=PACK),
@@ -148,73 +130,144 @@ def tile_gcn_s_kernel(tc, seq, adj, W, b, alpha, out):
             )
             h_grouped_of.append(h_grouped)
 
-        def transpose_adj(k):
+        def quantise_h(g):
+            h_codes = per_graph.tile([P, F_OUT], U32, align_bytes=64)
+            h_scales = per_graph.tile([P, F_OUT], U8, align_bytes=64)
+            nc.vector.quantize_mx(
+                out=h_codes[:].bitcast(FP8X4), scales=h_scales[:], in_=h_grouped_of[g][:]
+            )
+            h_codes_of.append(h_codes)
+            h_scales_of.append(h_scales)
+
+        def transpose_adj(k, tiles):
             adj_words = adj_rows_of[k][:].bitcast(F32)
             adj_t_ps = psum_t.tile([P, BANK], F32, tag="transposed")
-            for j in range(TILES_PER_HALF):
+            block = 0
+            for j in tiles:
                 for u in range(2):
-                    block = 2 * j + u
                     nc.tensor.transpose(
                         adj_t_ps[:, block * P : (block + 1) * P],
                         adj_words[:, j * 2 * P + u : (j + 1) * 2 * P : 2],
                         ident[:],
                     )
-            adj_grouped = per_half.tile([P, TILES_PER_HALF * P * PACK], BF16, align_bytes=64)
-            nc.scalar.copy(
-                out=adj_grouped[:].bitcast(F32).rearrange("p (j c u) -> p j c u", j=TILES_PER_HALF, u=2),
-                in_=adj_t_ps[:].rearrange("p (j u c) -> p j c u", j=TILES_PER_HALF, u=2),
-            )
-            adj_grouped_of.append(adj_grouped)
+                    block += 1
+            return adj_t_ps
 
-        def quantise(k):
-            adj_codes = per_half.tile([P, TILES_PER_HALF * P], U32, align_bytes=64)
-            adj_scales = per_half.tile([P, TILES_PER_HALF * P], U8, align_bytes=64)
+        def group_adj(copy, adj_t_ps, tiles):
+            n = len(tiles)
+            adj_grouped = per_half.tile(
+                [P, n * P * PACK], BF16, align_bytes=64, tag="adj_grouped%d" % n
+            )
+            copy(
+                out=adj_grouped[:].bitcast(F32).rearrange("p (j c u) -> p j c u", j=n, u=2),
+                in_=adj_t_ps[:, 0 : n * 2 * P].rearrange("p (j u c) -> p j c u", j=n, u=2),
+            )
+            return adj_grouped
+
+        def quantise_adj(k, adj_grouped, tiles):
+            n = len(tiles)
+            adj_codes = per_half.tile([P, n * P], U32, align_bytes=64, tag="adj_codes%d" % n)
+            adj_scales = per_half.tile([P, n * P], U8, align_bytes=64, tag="adj_scales%d" % n)
             nc.vector.quantize_mx(
-                out=adj_codes[:].bitcast(FP8X4), scales=adj_scales[:], in_=adj_grouped_of[k][:]
+                out=adj_codes[:].bitcast(FP8X4), scales=adj_scales[:], in_=adj_grouped[:]
             )
-            adj_codes_of.append(adj_codes)
-            adj_scales_of.append(adj_scales)
-            if k % 2 == 0:
-                h_codes = per_graph.tile([P, F_OUT], U32, align_bytes=64)
-                h_scales = per_graph.tile([P, F_OUT], U8, align_bytes=64)
-                nc.vector.quantize_mx(
-                    out=h_codes[:].bitcast(FP8X4), scales=h_scales[:], in_=h_grouped_of[k // 2][:]
-                )
-                h_codes_of.append(h_codes)
-                h_scales_of.append(h_scales)
+            for i, j in enumerate(tiles):
+                adj_codes_of[k, j] = adj_codes[:, i * P : (i + 1) * P]
+                adj_scales_of[k, j] = adj_scales[:, i * P : (i + 1) * P]
 
-        for k in range(HALVES):
-            if k % 2 == 0:
-                project(k // 2)
-            transpose_adj(k)
-            if k >= 1:
-                quantise(k - 1)
-        quantise(HALVES - 1)
-
-        for k in range(HALVES):
-            g = k // 2
-            a_ps = psum_acc.tile([P, TILES_PER_HALF * F_OUT], F32, tag="acc")
-            for j in range(TILES_PER_HALF):
+        def multiply(tiles, a_ps):
+            for i, (k, j) in enumerate(tiles):
                 nc.tensor.matmul_mx(
-                    out=a_ps[:, j * F_OUT : (j + 1) * F_OUT],
-                    lhsT=adj_codes_of[k][:, j * P : (j + 1) * P].bitcast(FP8X4),
-                    lhsT_scale=adj_scales_of[k][:, j * P : (j + 1) * P],
-                    rhs=h_codes_of[g][:].bitcast(FP8X4),
-                    rhs_scale=h_scales_of[g][:],
+                    out=a_ps[:, i * F_OUT : (i + 1) * F_OUT],
+                    lhsT=adj_codes_of[k, j].bitcast(FP8X4),
+                    lhsT_scale=adj_scales_of[k, j],
+                    rhs=h_codes_of[k // 2][:].bitcast(FP8X4),
+                    rhs_scale=h_scales_of[k // 2][:],
                     start=True,
                     stop=True,
                 )
-            neg_part = per_half.tile([P, TILES_PER_HALF * F_OUT], F32)
-            nc.scalar.activation(out=neg_part[:], in_=a_ps[:], func=ACT.Relu, scale=-1.0)
-            result = per_half.tile([P, TILES_PER_HALF * F_OUT], F32)
+
+        def negative_part(a_ps, width):
+            neg_part = per_half.tile([P, width], F32, tag="neg%d" % width)
+            nc.scalar.activation(out=neg_part[:], in_=a_ps[:, 0:width], func=ACT.Relu, scale=-1.0)
+            return neg_part
+
+        def prelu(result, a_ps, neg_part, width):
             nc.vector.scalar_tensor_tensor(
-                out=result[:],
+                out=result,
                 in0=neg_part[:],
                 scalar=one_minus_alpha[:, 0:1],
-                in1=a_ps[:],
+                in1=a_ps[:, 0:width],
                 op0=ALU.mult,
                 op1=ALU.add,
             )
-            out_view = out[g].rearrange("(p j) o -> p (j o)", j=ROW_TILES)
-            first = (k % 2) * TILES_PER_HALF * F_OUT
-            nc.sync.dma_start(out=out_view[:, first : first + TILES_PER_HALF * F_OUT], in_=result[:])
+
+        warm(WARM_HEAD)
+        w_t_ps = psum_t.tile([P, BANK], F32, tag="transposed")
+        nc.tensor.transpose(w_t_ps[:, 0:P], w_rows[:].bitcast(F32), ident[:])
+        w_t = const.tile([P, F_OUT], F32)
+        nc.scalar.copy(out=w_t[:], in_=w_t_ps[:, 0:P])
+        w_pairs = w_t[:].bitcast(BF16).rearrange("p (o r) -> p o r", r=2)
+        nc.vector.tensor_copy(out=small_row[0:1, 0 : F_OUT + 1], in_=b_alpha[:])
+
+        both = range(TILES_PER_HALF)
+        v_copy = nc.vector.tensor_copy
+        s_copy = nc.scalar.copy
+
+        transpose_seq(0, [s_copy, v_copy])
+        transpose_seq(1, [s_copy, v_copy])
+
+        warm(WARM_GAP)
+        small_ps = psum_t.tile([P, BANK], F32, tag="transposed")
+        nc.tensor.matmul(small_ps[:, 0 : 2 * F_OUT], lhsT=ones[:], rhs=small_row[:], start=True, stop=True)
+        bias_all = const.tile([P, F_OUT], F32)
+        nc.vector.tensor_copy(out=bias_all[:], in_=small_ps[:, 0:F_OUT])
+        one_minus_alpha = const.tile([P, 1], F32)
+        nc.vector.tensor_scalar(
+            out=one_minus_alpha[:],
+            in0=small_ps[:, F_OUT : F_OUT + 1],
+            scalar1=-1.0,
+            scalar2=1.0,
+            op0=ALU.mult,
+            op1=ALU.add,
+        )
+
+        h0 = project(0)
+        add_bias(h0)
+        t0 = transpose_adj(0, both)
+        g0 = group_adj(s_copy, t0, both)
+        h1 = project(1)
+        quantise_h(0)
+        add_bias(h1)
+        t1 = transpose_adj(1, both)
+        g1 = group_adj(s_copy, t1, both)
+        quantise_adj(0, g0, both)
+        t2 = transpose_adj(2, both)
+        g2 = group_adj(s_copy, t2, both)
+        quantise_adj(1, g1, both)
+        quantise_h(1)
+        t30 = transpose_adj(3, [0])
+        g30 = group_adj(s_copy, t30, [0])
+        t31 = transpose_adj(3, [1])
+        g31 = group_adj(s_copy, t31, [1])
+        quantise_adj(2, g2, both)
+        quantise_adj(3, g30, [0])
+        quantise_adj(3, g31, [1])
+
+        out_view = [out[g].rearrange("(p j) o -> p (j o)", j=ROW_TILES) for g in range(GRAPHS)]
+        for k in range(HALVES):
+            g = k // 2
+            result = per_half.tile([P, 2 * F_OUT], F32)
+            groups = [[0, 1]] if k < HALVES - 1 else [[0], [1]]
+            for tiles in groups:
+                width = len(tiles) * F_OUT
+                first = tiles[0] * F_OUT
+                if k < HALVES - 1:
+                    a_ps = psum_acc.tile([P, BANK], F32, tag="acc")
+                else:
+                    a_ps = psum_t.tile([P, BANK], F32, tag="transposed")
+                multiply([(k, j) for j in tiles], a_ps)
+                neg_part = negative_part(a_ps, width)
+                prelu(result[:, first : first + width], a_ps, neg_part, width)
+            first = (k % 2) * 2 * F_OUT
+            nc.sync.dma_start(out=out_view[g][:, first : first + 2 * F_OUT], in_=result[:])

@@ -18,8 +18,7 @@ ROW_TILES = NODES // P
 HALVES = 2 * GRAPHS
 TILES_PER_HALF = ROW_TILES // 2
 BANK = 512
-WARM_HEAD = 7
-WARM_GAP = 3
+WARM_PASSES = 11
 
 FLOPS = 2 * GRAPHS * NODES * F_IN * F_OUT + 2 * GRAPHS * NODES * NODES * F_OUT
 
@@ -41,17 +40,25 @@ def tile_gcn_s_kernel(tc, seq, adj, W, b, alpha, out):
         nc.sync.dma_start(out=w_rows[:], in_=W[:, :])
         seq_rows_of = []
         adj_rows_of = []
-        for g in range(GRAPHS):
+
+        def load_seq(g):
             seq_rows = per_graph.tile([P, PACK * F_IN], BF16)
             nc.sync.dma_start(out=seq_rows[:], in_=seq[g].rearrange("(p t) i -> p (t i)", t=PACK))
             seq_rows_of.append(seq_rows)
-        for g in range(GRAPHS):
-            adj_view = adj[g].rearrange("(p j) m -> p (j m)", j=ROW_TILES)
-            for half in range(2):
-                adj_rows = per_half.tile([P, TILES_PER_HALF * NODES], BF16)
-                first = half * TILES_PER_HALF * NODES
-                nc.sync.dma_start(out=adj_rows[:], in_=adj_view[:, first : first + TILES_PER_HALF * NODES])
-                adj_rows_of.append(adj_rows)
+
+        def load_adj(k):
+            adj_rows = per_half.tile([P, TILES_PER_HALF * NODES], BF16)
+            adj_view = adj[k // 2].rearrange("(p j) m -> p (j m)", j=ROW_TILES)
+            first = (k % 2) * TILES_PER_HALF * NODES
+            nc.sync.dma_start(out=adj_rows[:], in_=adj_view[:, first : first + TILES_PER_HALF * NODES])
+            adj_rows_of.append(adj_rows)
+
+        load_seq(0)
+        load_adj(0)
+        load_seq(1)
+        load_adj(1)
+        load_adj(2)
+        load_adj(3)
 
         warm_zeros = const.tile([P, P * PACK], BF16, align_bytes=64)
         nc.vector.memset(warm_zeros[:].bitcast(F32), 0.0)
@@ -202,7 +209,7 @@ def tile_gcn_s_kernel(tc, seq, adj, W, b, alpha, out):
                 op1=ALU.add,
             )
 
-        warm(WARM_HEAD)
+        warm(WARM_PASSES)
         w_t_ps = psum_t.tile([P, BANK], F32, tag="transposed")
         nc.tensor.transpose(w_t_ps[:, 0:P], w_rows[:].bitcast(F32), ident[:])
         w_t = const.tile([P, F_OUT], F32)
@@ -215,9 +222,6 @@ def tile_gcn_s_kernel(tc, seq, adj, W, b, alpha, out):
         s_copy = nc.scalar.copy
 
         transpose_seq(0, [s_copy, v_copy])
-        transpose_seq(1, [s_copy, v_copy])
-
-        warm(WARM_GAP)
         small_ps = psum_t.tile([P, BANK], F32, tag="transposed")
         nc.tensor.matmul(small_ps[:, 0 : 2 * F_OUT], lhsT=ones[:], rhs=small_row[:], start=True, stop=True)
         bias_all = const.tile([P, F_OUT], F32)
@@ -231,20 +235,20 @@ def tile_gcn_s_kernel(tc, seq, adj, W, b, alpha, out):
             op0=ALU.mult,
             op1=ALU.add,
         )
-
-        h0 = project(0)
-        add_bias(h0)
         t0 = transpose_adj(0, both)
         g0 = group_adj(s_copy, t0, both)
-        h1 = project(1)
-        quantise_h(0)
-        add_bias(h1)
+        h0 = project(0)
+        add_bias(h0)
+        transpose_seq(1, [s_copy, s_copy])
+        quantise_adj(0, g0, both)
         t1 = transpose_adj(1, both)
         g1 = group_adj(s_copy, t1, both)
-        quantise_adj(0, g0, both)
+        quantise_h(0)
+        h1 = project(1)
+        add_bias(h1)
+        quantise_adj(1, g1, both)
         t2 = transpose_adj(2, both)
         g2 = group_adj(s_copy, t2, both)
-        quantise_adj(1, g1, both)
         quantise_h(1)
         t30 = transpose_adj(3, [0])
         g30 = group_adj(s_copy, t30, [0])

@@ -17,6 +17,7 @@ GRAPHS, NODES, F_IN, F_OUT = 2, 512, 256, 128
 ROW_TILES = NODES // P
 HALVES = 2 * GRAPHS
 TILES_PER_HALF = ROW_TILES // 2
+SMALL = F_OUT + 2
 BANK = 512
 WARM_PASSES = 11
 
@@ -66,7 +67,7 @@ def tile_gcn_s_kernel(tc, seq, adj, W, b, alpha, out):
         warm_scales = const.tile([P, P], U8, align_bytes=64)
         nc.vector.quantize_mx(out=warm_codes[:].bitcast(FP8X4), scales=warm_scales[:], in_=warm_zeros[:])
 
-        small_row = const.tile([P, 2 * F_OUT], BF16)
+        small_row = const.tile([P, SMALL], BF16)
         nc.gpsimd.memset(small_row[:], 0.0)
         zero_col = const.tile([P, 1], F32)
         nc.gpsimd.memset(zero_col[:], 0.0)
@@ -223,7 +224,7 @@ def tile_gcn_s_kernel(tc, seq, adj, W, b, alpha, out):
 
         transpose_seq(0, [s_copy, v_copy])
         small_ps = psum_t.tile([P, BANK], F32, tag="transposed")
-        nc.tensor.matmul(small_ps[:, 0 : 2 * F_OUT], lhsT=ones[:], rhs=small_row[:], start=True, stop=True)
+        nc.tensor.matmul(small_ps[:, 0:SMALL], lhsT=ones[:], rhs=small_row[:], start=True, stop=True)
         bias_all = const.tile([P, F_OUT], F32)
         nc.vector.tensor_copy(out=bias_all[:], in_=small_ps[:, 0:F_OUT])
         one_minus_alpha = const.tile([P, 1], F32)
@@ -237,9 +238,9 @@ def tile_gcn_s_kernel(tc, seq, adj, W, b, alpha, out):
         )
         t0 = transpose_adj(0, both)
         g0 = group_adj(s_copy, t0, both)
+        transpose_seq(1, [v_copy, v_copy])
         h0 = project(0)
         add_bias(h0)
-        transpose_seq(1, [s_copy, s_copy])
         quantise_adj(0, g0, both)
         t1 = transpose_adj(1, both)
         g1 = group_adj(s_copy, t1, both)

@@ -245,17 +245,17 @@ def tile_gcn_s_kernel(tc, seq, adj, W, b, alpha, out):
         t1 = transpose_adj(1, both)
         g1 = group_adj(s_copy, t1, both)
         quantise_h(0)
-        h1 = project(1)
-        add_bias(h1)
-        quantise_adj(1, g1, both)
         t2 = transpose_adj(2, both)
         g2 = group_adj(s_copy, t2, both)
-        quantise_h(1)
+        h1 = project(1)
+        quantise_adj(1, g1, both)
+        add_bias(h1)
         t30 = transpose_adj(3, [0])
         g30 = group_adj(s_copy, t30, [0])
         t31 = transpose_adj(3, [1])
         g31 = group_adj(s_copy, t31, [1])
         quantise_adj(2, g2, both)
+        quantise_h(1)
         quantise_adj(3, g30, [0])
         quantise_adj(3, g31, [1])
 

@@ -274,5 +274,5 @@ def tile_gcn_s_kernel(tc, seq, adj, W, b, alpha, out):
                 multiply([(k, j) for j in tiles], a_ps)
                 neg_part = negative_part(a_ps, width)
                 prelu(result[:, first : first + width], a_ps, neg_part, width)
-            first = (k % 2) * 2 * F_OUT
-            nc.sync.dma_start(out=out_view[g][:, first : first + 2 * F_OUT], in_=result[:])
+                to = (k % 2) * 2 * F_OUT + first
+                nc.sync.dma_start(out=out_view[g][:, to : to + width], in_=result[:, first : first + width])

@@ -263,7 +263,7 @@ def tile_gcn_s_kernel(tc, seq, adj, W, b, alpha, out):
         for k in range(HALVES):
             g = k // 2
             result = per_half.tile([P, 2 * F_OUT], F32)
-            groups = [[0, 1]] if k < HALVES - 1 else [[0], [1]]
+            groups = [[0, 1]] if k < 2 else [[0], [1]]
             for tiles in groups:
                 width = len(tiles) * F_OUT
                 first = tiles[0] * F_OUT

@@ -35,8 +35,6 @@ def tile_gcn_s_kernel(tc, seq, adj, W, b, alpha, out):
         psum_acc = ctx.enter_context(tc.psum_pool(name="psum_acc", bufs=4))
 
         b_alpha = const.tile([1, F_OUT + 1], BF16)
-        nc.scalar.dma_start(out=b_alpha[:, 0:F_OUT], in_=b.unsqueeze(0))
-        nc.scalar.dma_start(out=b_alpha[:, F_OUT : F_OUT + 1], in_=alpha.unsqueeze(0))
         w_rows = const.tile([P, F_IN], BF16)
         nc.sync.dma_start(out=w_rows[:], in_=W[:, :])
         seq_rows_of = []
@@ -55,6 +53,8 @@ def tile_gcn_s_kernel(tc, seq, adj, W, b, alpha, out):
             adj_rows_of.append(adj_rows)
 
         load_seq(0)
+        nc.sync.dma_start(out=b_alpha[:, 0:F_OUT], in_=b.unsqueeze(0))
+        nc.sync.dma_start(out=b_alpha[:, F_OUT : F_OUT + 1], in_=alpha.unsqueeze(0))
         load_adj(0)
         load_seq(1)
         load_adj(1)
@@ -260,8 +260,12 @@ def tile_gcn_s_kernel(tc, seq, adj, W, b, alpha, out):
         quantise_adj(3, g31, [1])
 
         out_view = [out[g].rearrange("(p j) o -> p (j o)", j=ROW_TILES) for g in range(GRAPHS)]
+
+        def store(k, result, first, width):
+            to = (k % 2) * TILES_PER_HALF * F_OUT + first
+            nc.sync.dma_start(out=out_view[k // 2][:, to : to + width], in_=result[:, first : first + width])
+
         for k in range(HALVES):
-            g = k // 2
             result = per_half.tile([P, 2 * F_OUT], F32)
             groups = [[0, 1]] if k < 2 else [[0], [1]]
             for tiles in groups:
@@ -274,5 +278,7 @@ def tile_gcn_s_kernel(tc, seq, adj, W, b, alpha, out):
                 multiply([(k, j) for j in tiles], a_ps)
                 neg_part = negative_part(a_ps, width)
                 prelu(result[:, first : first + width], a_ps, neg_part, width)
-                to = (k % 2) * 2 * F_OUT + first
-                nc.sync.dma_start(out=out_view[g][:, to : to + width], in_=result[:, first : first + width])
+                if k == HALVES - 1:
+                    store(k, result, first, width)
+            if k < HALVES - 1:
+                store(k, result, 0, TILES_PER_HALF * F_OUT)

@@ -31,8 +31,8 @@ def tile_gcn_s_kernel(tc, seq, adj, W, b, alpha, out):
         const = ctx.enter_context(tc.tile_pool(name="const", bufs=1))
         per_graph = ctx.enter_context(tc.tile_pool(name="per_graph", bufs=GRAPHS))
         per_half = ctx.enter_context(tc.tile_pool(name="per_half", bufs=HALVES))
-        psum_t = ctx.enter_context(tc.psum_pool(name="psum_t", bufs=4))
-        psum_acc = ctx.enter_context(tc.psum_pool(name="psum_acc", bufs=4))
+        psum_t = ctx.enter_context(tc.psum_pool(name="psum_t", bufs=5))
+        psum_acc = ctx.enter_context(tc.psum_pool(name="psum_acc", bufs=3))
 
         b_alpha = const.tile([1, F_OUT + 1], BF16)
         w_rows = const.tile([P, F_IN], BF16)
@@ -147,29 +147,26 @@ def tile_gcn_s_kernel(tc, seq, adj, W, b, alpha, out):
             h_codes_of.append(h_codes)
             h_scales_of.append(h_scales)
 
-        def transpose_adj(k, tiles):
+        def transpose_adj(k, j):
             adj_words = adj_rows_of[k][:].bitcast(F32)
             adj_t_ps = psum_t.tile([P, BANK], F32, tag="transposed")
-            block = 0
-            for j in tiles:
-                for u in range(2):
-                    nc.tensor.transpose(
-                        adj_t_ps[:, block * P : (block + 1) * P],
-                        adj_words[:, j * 2 * P + u : (j + 1) * 2 * P : 2],
-                        ident[:],
-                    )
-                    block += 1
+            for u in range(2):
+                nc.tensor.transpose(
+                    adj_t_ps[:, u * P : (u + 1) * P],
+                    adj_words[:, j * 2 * P + u : (j + 1) * 2 * P : 2],
+                    ident[:],
+                )
             return adj_t_ps
 
-        def group_adj(copy, adj_t_ps, tiles):
-            n = len(tiles)
-            adj_grouped = per_half.tile(
-                [P, n * P * PACK], BF16, align_bytes=64, tag="adj_grouped%d" % n
-            )
-            copy(
-                out=adj_grouped[:].bitcast(F32).rearrange("p (j c u) -> p j c u", j=n, u=2),
-                in_=adj_t_ps[:, 0 : n * 2 * P].rearrange("p (j u c) -> p j c u", j=n, u=2),
-            )
+        def group_adj(k):
+            adj_grouped = per_half.tile([P, TILES_PER_HALF * P * PACK], BF16, align_bytes=64)
+            for j in range(TILES_PER_HALF):
+                adj_t_ps = transpose_adj(k, j)
+                words = adj_grouped[:, j * P * PACK : (j + 1) * P * PACK].bitcast(F32)
+                nc.scalar.copy(
+                    out=words.rearrange("p (c u) -> p c u", u=2),
+                    in_=adj_t_ps[:, 0 : 2 * P].rearrange("p (u c) -> p c u", u=2),
+                )
             return adj_grouped
 
         def quantise_adj(k, adj_grouped, tiles):
@@ -177,7 +174,9 @@ def tile_gcn_s_kernel(tc, seq, adj, W, b, alpha, out):
             adj_codes = per_half.tile([P, n * P], U32, align_bytes=64, tag="adj_codes%d" % n)
             adj_scales = per_half.tile([P, n * P], U8, align_bytes=64, tag="adj_scales%d" % n)
             nc.vector.quantize_mx(
-                out=adj_codes[:].bitcast(FP8X4), scales=adj_scales[:], in_=adj_grouped[:]
+                out=adj_codes[:].bitcast(FP8X4),
+                scales=adj_scales[:],
+                in_=adj_grouped[:, tiles[0] * P * PACK : (tiles[0] + n) * P * PACK],
             )
             for i, j in enumerate(tiles):
                 adj_codes_of[k, j] = adj_codes[:, i * P : (i + 1) * P]
@@ -236,28 +235,22 @@ def tile_gcn_s_kernel(tc, seq, adj, W, b, alpha, out):
             op0=ALU.mult,
             op1=ALU.add,
         )
-        t0 = transpose_adj(0, both)
-        g0 = group_adj(s_copy, t0, both)
+        g0 = group_adj(0)
         transpose_seq(1, [v_copy, v_copy])
         h0 = project(0)
         add_bias(h0)
         quantise_adj(0, g0, both)
-        t1 = transpose_adj(1, both)
-        g1 = group_adj(s_copy, t1, both)
+        g1 = group_adj(1)
         quantise_h(0)
-        t2 = transpose_adj(2, both)
-        g2 = group_adj(s_copy, t2, both)
         h1 = project(1)
-        quantise_adj(1, g1, both)
         add_bias(h1)
-        t30 = transpose_adj(3, [0])
-        g30 = group_adj(s_copy, t30, [0])
-        t31 = transpose_adj(3, [1])
-        g31 = group_adj(s_copy, t31, [1])
-        quantise_adj(2, g2, both)
+        quantise_adj(1, g1, both)
         quantise_h(1)
-        quantise_adj(3, g30, [0])
-        quantise_adj(3, g31, [1])
+        g2 = group_adj(2)
+        g3 = group_adj(3)
+        quantise_adj(2, g2, both)
+        quantise_adj(3, g3, [0])
+        quantise_adj(3, g3, [1])
 
         out_view = [out[g].rearrange("(p j) o -> p (j o)", j=ROW_TILES) for g in range(GRAPHS)]
 
@@ -271,7 +264,7 @@ def tile_gcn_s_kernel(tc, seq, adj, W, b, alpha, out):
             for tiles in groups:
                 width = len(tiles) * F_OUT
                 first = tiles[0] * F_OUT
-                if k < HALVES - 1:
+                if k < 2:
                     a_ps = psum_acc.tile([P, BANK], F32, tag="acc")
                 else:
                     a_ps = psum_t.tile([P, BANK], F32, tag="transposed")

@@ -19,7 +19,7 @@ HALVES = 2 * GRAPHS
 TILES_PER_HALF = ROW_TILES // 2
 SMALL = F_OUT + 2
 BANK = 512
-WARM_PASSES = 11
+WARM_PASSES = 10
 
 FLOPS = 2 * GRAPHS * NODES * F_IN * F_OUT + 2 * GRAPHS * NODES * NODES * F_OUT
 

from contextlib import ExitStack

import concourse.mybir as mybir
from concourse.masks import make_identity

F32 = mybir.dt.float32
BF16 = mybir.dt.bfloat16
U32 = mybir.dt.uint32
U8 = mybir.dt.uint8
FP8X4 = mybir.dt.float8_e4m3fn_x4
ALU = mybir.AluOpType
ACT = mybir.ActivationFunctionType

P = 128
PACK = 4
GRAPHS, NODES, F_IN, F_OUT = 2, 512, 256, 128
ROW_TILES = NODES // P
HALVES = 2 * GRAPHS
TILES_PER_HALF = ROW_TILES // 2
SMALL = F_OUT + 2
BANK = 512
WARM_PASSES = 10

FLOPS = 2 * GRAPHS * NODES * F_IN * F_OUT + 2 * GRAPHS * NODES * NODES * F_OUT


def tile_gcn_s_kernel(tc, seq, adj, W, b, alpha, out):
    nc = tc.nc
    with ExitStack() as ctx:
        ctx.enter_context(tc.manual_schedule())
        const = ctx.enter_context(tc.tile_pool(name="const", bufs=1))
        per_graph = ctx.enter_context(tc.tile_pool(name="per_graph", bufs=GRAPHS))
        per_half = ctx.enter_context(tc.tile_pool(name="per_half", bufs=HALVES))
        psum_t = ctx.enter_context(tc.psum_pool(name="psum_t", bufs=5))
        psum_acc = ctx.enter_context(tc.psum_pool(name="psum_acc", bufs=3))

        b_alpha = const.tile([1, F_OUT + 1], BF16)
        w_rows = const.tile([P, F_IN], BF16)
        nc.sync.dma_start(out=w_rows[:], in_=W[:, :])
        seq_rows_of = []
        adj_rows_of = []

        def load_seq(g):
            seq_rows = per_graph.tile([P, PACK * F_IN], BF16)
            nc.sync.dma_start(out=seq_rows[:], in_=seq[g].rearrange("(p t) i -> p (t i)", t=PACK))
            seq_rows_of.append(seq_rows)

        def load_adj(k):
            adj_rows = per_half.tile([P, TILES_PER_HALF * NODES], BF16)
            adj_view = adj[k // 2].rearrange("(p j) m -> p (j m)", j=ROW_TILES)
            first = (k % 2) * TILES_PER_HALF * NODES
            nc.sync.dma_start(out=adj_rows[:], in_=adj_view[:, first : first + TILES_PER_HALF * NODES])
            adj_rows_of.append(adj_rows)

        load_seq(0)
        nc.sync.dma_start(out=b_alpha[:, 0:F_OUT], in_=b.unsqueeze(0))
        nc.sync.dma_start(out=b_alpha[:, F_OUT : F_OUT + 1], in_=alpha.unsqueeze(0))
        load_adj(0)
        load_seq(1)
        load_adj(1)
        load_adj(2)
        load_adj(3)

        warm_zeros = const.tile([P, P * PACK], BF16, align_bytes=64)
        nc.vector.memset(warm_zeros[:].bitcast(F32), 0.0)
        warm_codes = const.tile([P, P], U32, align_bytes=64)
        warm_scales = const.tile([P, P], U8, align_bytes=64)
        nc.vector.quantize_mx(out=warm_codes[:].bitcast(FP8X4), scales=warm_scales[:], in_=warm_zeros[:])

        small_row = const.tile([P, SMALL], BF16)
        nc.gpsimd.memset(small_row[:], 0.0)
        zero_col = const.tile([P, 1], F32)
        nc.gpsimd.memset(zero_col[:], 0.0)
        ident = const.tile([P, P], F32)
        make_identity(nc, ident[:])
        ones = const.tile([P, P], BF16)
        nc.scalar.activation(
            out=ones[:], in_=zero_col[:, 0:1].to_broadcast([P, P]), func=ACT.Relu, scale=0.0, bias=1.0
        )

        warm_ps = psum_acc.tile([P, BANK], F32, tag="acc")

        def warm(passes):
            for i in range(passes):
                nc.tensor.matmul_mx(
                    out=warm_ps[:, 0:P],
                    lhsT=warm_codes[:].bitcast(FP8X4),
                    lhsT_scale=warm_scales[:],
                    rhs=warm_codes[:].bitcast(FP8X4),
                    rhs_scale=warm_scales[:],
                    start=True,
                    stop=True,
                )

        seq_t_of = []
        h_grouped_of = []
        h_codes_of = []
        h_scales_of = []
        adj_codes_of = {}
        adj_scales_of = {}

        def transpose_seq(g, copies):
            seq_words = seq_rows_of[g][:].bitcast(F32)
            for u in range(2):
                seq_t_ps = psum_t.tile([P, BANK], F32, tag="transposed")
                for e in range(2):
                    t = 2 * u + e
                    nc.tensor.transpose(
                        seq_t_ps[:, e * P : (e + 1) * P], seq_words[:, t * P : (t + 1) * P], ident[:]
                    )
                seq_t = per_half.tile([P, 2 * P], F32)
                copies[u](out=seq_t[:], in_=seq_t_ps[:, 0 : 2 * P])
                seq_t_of.append(seq_t)

        def project(g):
            h_ps = psum_acc.tile([P, PACK * F_OUT], F32, tag="acc")
            for t in range(PACK):
                seq_pairs = seq_t_of[2 * g + t // 2][:].bitcast(BF16).rearrange(
                    "p (e c r) -> p e c r", e=2, r=2
                )
                for r in range(2):
                    nc.tensor.matmul(
                        h_ps[:, t * F_OUT : (t + 1) * F_OUT],
                        lhsT=seq_pairs[:, t % 2, :, r],
                        rhs=w_pairs[:, :, r],
                        start=(r == 0),
                        stop=(r == 1),
                    )
            return h_ps

        def add_bias(h_ps):
            h_grouped = per_graph.tile([P, F_OUT * PACK], BF16, align_bytes=64)
            nc.vector.tensor_tensor(
                out=h_grouped[:].rearrange("p (o t) -> p o t", t=PACK),
                in0=h_ps[:].rearrange("p (t o) -> p o t", t=PACK),
                in1=bias_all[:].unsqueeze(2).to_broadcast([P, F_OUT, PACK]),
                op=ALU.add,
            )
            h_grouped_of.append(h_grouped)

        def quantise_h(g):
            h_codes = per_graph.tile([P, F_OUT], U32, align_bytes=64)
            h_scales = per_graph.tile([P, F_OUT], U8, align_bytes=64)
            nc.vector.quantize_mx(
                out=h_codes[:].bitcast(FP8X4), scales=h_scales[:], in_=h_grouped_of[g][:]
            )
            h_codes_of.append(h_codes)
            h_scales_of.append(h_scales)

        def transpose_adj(k, j):
            adj_words = adj_rows_of[k][:].bitcast(F32)
            adj_t_ps = psum_t.tile([P, BANK], F32, tag="transposed")
            for u in range(2):
                nc.tensor.transpose(
                    adj_t_ps[:, u * P : (u + 1) * P],
                    adj_words[:, j * 2 * P + u : (j + 1) * 2 * P : 2],
                    ident[:],
                )
            return adj_t_ps

        def group_adj(k):
            adj_grouped = per_half.tile([P, TILES_PER_HALF * P * PACK], BF16, align_bytes=64)
            for j in range(TILES_PER_HALF):
                adj_t_ps = transpose_adj(k, j)
                words = adj_grouped[:, j * P * PACK : (j + 1) * P * PACK].bitcast(F32)
                nc.scalar.copy(
                    out=words.rearrange("p (c u) -> p c u", u=2),
                    in_=adj_t_ps[:, 0 : 2 * P].rearrange("p (u c) -> p c u", u=2),
                )
            return adj_grouped

        def quantise_adj(k, adj_grouped, tiles):
            n = len(tiles)
            adj_codes = per_half.tile([P, n * P], U32, align_bytes=64, tag="adj_codes%d" % n)
            adj_scales = per_half.tile([P, n * P], U8, align_bytes=64, tag="adj_scales%d" % n)
            nc.vector.quantize_mx(
                out=adj_codes[:].bitcast(FP8X4),
                scales=adj_scales[:],
                in_=adj_grouped[:, tiles[0] * P * PACK : (tiles[0] + n) * P * PACK],
            )
            for i, j in enumerate(tiles):
                adj_codes_of[k, j] = adj_codes[:, i * P : (i + 1) * P]
                adj_scales_of[k, j] = adj_scales[:, i * P : (i + 1) * P]

        def multiply(tiles, a_ps):
            for i, (k, j) in enumerate(tiles):
                nc.tensor.matmul_mx(
                    out=a_ps[:, i * F_OUT : (i + 1) * F_OUT],
                    lhsT=adj_codes_of[k, j].bitcast(FP8X4),
                    lhsT_scale=adj_scales_of[k, j],
                    rhs=h_codes_of[k // 2][:].bitcast(FP8X4),
                    rhs_scale=h_scales_of[k // 2][:],
                    start=True,
                    stop=True,
                )

        def negative_part(a_ps, width):
            neg_part = per_half.tile([P, width], F32, tag="neg%d" % width)
            nc.scalar.activation(out=neg_part[:], in_=a_ps[:, 0:width], func=ACT.Relu, scale=-1.0)
            return neg_part

        def prelu(result, a_ps, neg_part, width):
            nc.vector.scalar_tensor_tensor(
                out=result,
                in0=neg_part[:],
                scalar=one_minus_alpha[:, 0:1],
                in1=a_ps[:, 0:width],
                op0=ALU.mult,
                op1=ALU.add,
            )

        warm(WARM_PASSES)
        w_t_ps = psum_t.tile([P, BANK], F32, tag="transposed")
        nc.tensor.transpose(w_t_ps[:, 0:P], w_rows[:].bitcast(F32), ident[:])
        w_t = const.tile([P, F_OUT], F32)
        nc.scalar.copy(out=w_t[:], in_=w_t_ps[:, 0:P])
        w_pairs = w_t[:].bitcast(BF16).rearrange("p (o r) -> p o r", r=2)
        nc.vector.tensor_copy(out=small_row[0:1, 0 : F_OUT + 1], in_=b_alpha[:])

        both = range(TILES_PER_HALF)
        v_copy = nc.vector.tensor_copy
        s_copy = nc.scalar.copy

        transpose_seq(0, [s_copy, v_copy])
        small_ps = psum_t.tile([P, BANK], F32, tag="transposed")
        nc.tensor.matmul(small_ps[:, 0:SMALL], lhsT=ones[:], rhs=small_row[:], start=True, stop=True)
        bias_all = const.tile([P, F_OUT], F32)
        nc.vector.tensor_copy(out=bias_all[:], in_=small_ps[:, 0:F_OUT])
        one_minus_alpha = const.tile([P, 1], F32)
        nc.vector.tensor_scalar(
            out=one_minus_alpha[:],
            in0=small_ps[:, F_OUT : F_OUT + 1],
            scalar1=-1.0,
            scalar2=1.0,
            op0=ALU.mult,
            op1=ALU.add,
        )
        g0 = group_adj(0)
        transpose_seq(1, [v_copy, v_copy])
        h0 = project(0)
        add_bias(h0)
        quantise_adj(0, g0, both)
        g1 = group_adj(1)
        quantise_h(0)
        h1 = project(1)
        add_bias(h1)
        quantise_adj(1, g1, both)
        quantise_h(1)
        g2 = group_adj(2)
        g3 = group_adj(3)
        quantise_adj(2, g2, both)
        quantise_adj(3, g3, [0])
        quantise_adj(3, g3, [1])

        out_view = [out[g].rearrange("(p j) o -> p (j o)", j=ROW_TILES) for g in range(GRAPHS)]

        def store(k, result, first, width):
            to = (k % 2) * TILES_PER_HALF * F_OUT + first
            nc.sync.dma_start(out=out_view[k // 2][:, to : to + width], in_=result[:, first : first + width])

        for k in range(HALVES):
            result = per_half.tile([P, 2 * F_OUT], F32)
            groups = [[0, 1]] if k < 2 else [[0], [1]]
            for tiles in groups:
                width = len(tiles) * F_OUT
                first = tiles[0] * F_OUT
                if k < 2:
                    a_ps = psum_acc.tile([P, BANK], F32, tag="acc")
                else:
                    a_ps = psum_t.tile([P, BANK], F32, tag="transposed")
                multiply([(k, j) for j in tiles], a_ps)
                neg_part = negative_part(a_ps, width)
                prelu(result[:, first : first + width], a_ps, neg_part, width)
                if k == HALVES - 1:
                    store(k, result, first, width)
            if k < HALVES - 1:
                store(k, result, 0, TILES_PER_HALF * F_OUT)
